import numpy as np
import ml_dtypes


def mxq(x, axis, fmt="e4m3"):
    dtype, down = {"e4m3": (ml_dtypes.float8_e4m3fn, 7), "e5m2": (ml_dtypes.float8_e5m2, 14)}[fmt]
    v = np.moveaxis(np.asarray(x, np.float32).astype(ml_dtypes.bfloat16).astype(np.float64), axis, -1)
    blocks = v.reshape(v.shape[:-1] + (-1, 32))
    amax = np.abs(blocks).max(-1, keepdims=True)
    byte = np.maximum(np.where(amax > 0, np.frexp(amax)[1] - 1 + 127, 0) - down, 1)
    scale = np.exp2(byte - 127.0)
    codes = (blocks / scale).astype(np.float32).astype(dtype).astype(np.float64)
    return np.moveaxis((codes * scale).reshape(v.shape), -1, axis)


WIDE = False


def mx_kscale(k):
    if not WIDE:
        return np.ones(k)
    levels = np.array([10, -10, 5, -5, 0])
    a = np.random.permutation(np.resize(levels, k // 512 * 4)).reshape(k // 512, 4)
    idx = np.arange(k)
    return np.exp2(a[idx // 512, idx % 128 // 32])


BF16 = ml_dtypes.bfloat16


def bf(x):
    return np.asarray(x, np.float32).astype(BF16)


def f64(x):
    return np.asarray(x).astype(np.float64)


E2M1 = np.array([0.0, 0.5, 1.0, 1.5, 2.0, 3.0, 4.0, 6.0, -0.0, -0.5, -1.0, -1.5, -2.0, -3.0, -4.0, -6.0])


def pack_weight(w, fmt):
    k, n = w.shape
    w = f64(bf(w)).reshape(k // 32, 32, n)
    amax = np.abs(w).max(1)
    if fmt == "e4m3":
        byte = np.frexp(amax)[1] - 1 + 127 - 7
    else:
        mant, ex = np.frexp(amax / 6.0)
        byte = np.where(mant > 0.5, ex, ex - 1) + 127
    byte = np.clip(np.where(amax > 0, byte, 1), 1, 254)
    scaled = (w * np.exp2(127.0 - byte)[:, None, :]).reshape(k, n).astype(np.float32)
    by_word = np.ascontiguousarray(scaled.reshape(k // 512, 128, 4, n).transpose(0, 1, 3, 2))
    if fmt == "e4m3":
        words = by_word.astype(ml_dtypes.float8_e4m3fn).view(np.uint8)
    else:
        c = by_word.astype(ml_dtypes.float4_e2m1fn).view(np.uint8) & 0xF
        words = c[..., 0::2] | (c[..., 1::2] << 4)
    return np.ascontiguousarray(words), np.ascontiguousarray(byte.astype(np.uint8).reshape(k // 512, 16, n))


def unpack_weight(words, scales, fmt):
    g, p, n, _ = words.shape
    if fmt == "e4m3":
        vals = np.ascontiguousarray(words).view(ml_dtypes.float8_e4m3fn).astype(np.float64)
    else:
        nib = np.empty((g, p, n, 4), np.uint8)
        nib[..., 0::2] = words & 0xF
        nib[..., 1::2] = words >> 4
        vals = E2M1[nib]
    vals = vals * np.repeat(np.exp2(scales.astype(np.float64) - 127.0), 8, axis=1)[..., None]
    return vals.transpose(0, 1, 3, 2).reshape(g * 512, n)


B, D_IN, D_OUT = 512, 2048, 2048
EPS = 0.01
FMT = "e4m3"


def setup_inputs():
    s, t = mx_kscale(D_IN), mx_kscale(D_OUT)
    x = bf(np.random.standard_normal((B, D_IN)) * s)
    W = np.random.standard_normal((D_OUT, D_IN)) / np.sqrt(D_IN) / s[None, :] * t[:, None]
    W_words, W_scales = pack_weight(np.ascontiguousarray(W.T), FMT)
    b = bf(np.random.standard_normal(D_OUT) * 0.3 * t)
    g = np.random.standard_normal((D_OUT, D_OUT)) / np.sqrt(D_OUT) / t[None, :]
    g_words, g_scales = pack_weight(np.ascontiguousarray(g.T), FMT)
    g_bias = bf(np.random.standard_normal(D_OUT) * 0.3)
    return {"x": x,
            "W_words": W_words,
            "W_scales": W_scales,
            "b": b,
            "g_words": g_words,
            "g_scales": g_scales,
            "g_bias": g_bias}


def reference(x, W_words, W_scales, b, g_words, g_scales, g_bias):
    h = (mxq(f64(x), 1, "e4m3") @ unpack_weight(W_words, W_scales, FMT)) + f64(b)
    c = np.cos((mxq(h, 1, "e4m3") @ unpack_weight(g_words, g_scales, FMT)) + f64(g_bias))
    return np.where(np.abs(c) < EPS, -c, c)

@@ -1,0 +1,246 @@
+import math
+from contextlib import ExitStack
+
+import concourse.mybir as mybir
+from concourse.masks import make_identity
+
+FLOPS = 2 * 2 * 512 * 2048 * 2048
+
+F32 = mybir.dt.float32
+BF16 = mybir.dt.bfloat16
+I32 = mybir.dt.int32
+U32 = mybir.dt.uint32
+U8 = mybir.dt.uint8
+FP8X4 = mybir.dt.float8_e4m3fn_x4
+ALU = mybir.AluOpType
+ACT = mybir.ActivationFunctionType
+
+P = 128
+PACK = 4
+K_PASS = P * PACK
+CHUNK = 512
+BATCH, D = 512, 2048
+TILES = BATCH // P
+GROUPS_K = D // K_PASS
+CHUNKS = D // CHUNK
+EPS = 0.01
+
+TILE_SETS = ((0, 1), (2, 3))
+
+
+def tile_onehiddenlayer_kernel(tc, x, W_words, W_scales, b, g_words, g_scales, g_bias, out):
+    nc = tc.nc
+    with ExitStack() as ctx:
+        ctx.enter_context(tc.manual_schedule())
+        keep = ctx.enter_context(tc.tile_pool(name="keep", bufs=1))
+        stage = ctx.enter_context(tc.tile_pool(name="stage", bufs=4))
+        tail = ctx.enter_context(tc.tile_pool(name="tail", bufs=4))
+        sums = ctx.enter_context(tc.psum_pool(name="sums", bufs=4))
+        turned = ctx.enter_context(tc.psum_pool(name="turned", bufs=4))
+
+        w_planes = keep.tile([P, D], U8, align_bytes=64)
+        g_planes = keep.tile([P, D], U8, align_bytes=64)
+        b_rows = keep.tile([P, D], BF16)
+        g_bias_rows = keep.tile([P, D], BF16)
+        zero_col = keep.tile([P, 1], F32)
+        sin_col = keep.tile([P, 1], F32)
+        neg_eps = keep.tile([P, 1], F32)
+        ones = keep.tile([P, P], BF16)
+        ident_f32 = keep.tile([P, P], F32)
+        ident_bf16 = keep.tile([P, P], BF16)
+        b_sorted = keep.tile([P, CHUNKS, PACK, P], F32)
+        g_turns = keep.tile([P, D], F32)
+        x_rows = [keep.tile([P, D], BF16, name="x_rows%d" % m) for m in range(TILES)]
+        w_chunks = [keep.tile([P, GROUPS_K, CHUNK], U32, name="w_chunk%d" % j, align_bytes=64) for j in range(CHUNKS)]
+        g_chunks = [keep.tile([P, GROUPS_K, CHUNK], U32, name="g_chunk%d" % j, align_bytes=64) for j in range(CHUNKS)]
+        x_codes = [keep.tile([P, GROUPS_K, P], U32, name="x_codes%d" % m, align_bytes=64) for m in range(TILES)]
+        x_scales = [keep.tile([P, GROUPS_K, P], U8, name="x_scales%d" % m, align_bytes=64) for m in range(TILES)]
+        h_codes = [keep.tile([P, GROUPS_K, P], U32, name="h_codes%d" % m, align_bytes=64) for m in range(TILES)]
+        h_scales = [keep.tile([P, GROUPS_K, P], U8, name="h_scales%d" % m, align_bytes=64) for m in range(TILES)]
+
+        nc.vector.memset(b_rows[:].bitcast(I32), 0)
+        nc.vector.memset(w_planes[:].bitcast(I32), 0)
+        nc.vector.memset(g_bias_rows[:].bitcast(I32), 0)
+        nc.vector.memset(g_planes[:].bitcast(I32), 0)
+        nc.vector.memset(zero_col[:], 0.0)
+        nc.vector.memset(neg_eps[:], -EPS)
+        nc.gpsimd.memset(ones[:], 1.0)
+        make_identity(nc, ident_f32[:])
+        make_identity(nc, ident_bf16[:])
+
+        def load_planes(planes, scales):
+            for quadrant in range(4):
+                nc.sync.dma_start(
+                    out=planes[32 * quadrant : 32 * quadrant + 16, :].bitcast(I32),
+                    in_=scales[:, 4 * quadrant : 4 * quadrant + 4, :].bitcast(I32),
+                )
+
+        def load_chunk(chunk_tile, words, j):
+            by_partition = words.rearrange("g p n t -> p g (n t)")
+            nc.sync.dma_start(
+                out=chunk_tile[:].bitcast(I32),
+                in_=by_partition[:, :, PACK * CHUNK * j : PACK * CHUNK * (j + 1)].bitcast(I32),
+            )
+
+        def load_x(m):
+            nc.sync.dma_start(out=x_rows[m][:], in_=x[P * m : P * (m + 1), :])
+
+        nc.scalar.dma_start(out=b_rows[0:1, :], in_=b.unsqueeze(0))
+        nc.scalar.dma_start(out=g_bias_rows[0:1, :], in_=g_bias.unsqueeze(0))
+        load_planes(w_planes, W_scales)
+        for m in TILE_SETS[0]:
+            load_x(m)
+        for j in range(CHUNKS):
+            load_chunk(w_chunks[j], W_words, j)
+        load_x(TILE_SETS[1][0])
+        load_planes(g_planes, g_scales)
+        load_chunk(g_chunks[0], g_words, 0)
+        load_x(TILE_SETS[1][1])
+        for j in range(1, CHUNKS):
+            load_chunk(g_chunks[j], g_words, j)
+
+        nc.scalar.activation(out=sin_col[:], in_=zero_col[:], func=ACT.Sin)
+
+        def spread_chunk(rows, j):
+            spread = sums.tile([P, CHUNK], F32, tag="sum")
+            nc.tensor.matmul(out=spread[:], lhsT=ones[:], rhs=rows[:, CHUNK * j : CHUNK * (j + 1)], start=True, stop=True)
+            return spread
+
+        def turn_x(m):
+            words = x_rows[m][:].bitcast(F32)
+            grouped = stage.tile([P, GROUPS_K, P, PACK], BF16, align_bytes=64, tag="x_grouped")
+            for half in range(2):
+                bank = turned.tile([P, 2, 2, P], F32, tag="turned")
+                for g2 in range(2):
+                    g = 2 * half + g2
+                    for u in range(2):
+                        nc.tensor.transpose(bank[:, g2, u, :], words[:, 256 * g + u : 256 * (g + 1) : 2], ident_f32[:])
+                dst = grouped[:].bitcast(F32)[:, 2 * half : 2 * half + 2, :, :]
+                src = bank[:].rearrange("p g u r -> p g r u")
+                if half == 0:
+                    nc.scalar.copy(out=dst, in_=src)
+                else:
+                    nc.vector.tensor_copy(out=dst, in_=src)
+            return grouped
+
+        def quantise_x(m, grouped):
+            nc.vector.quantize_mx(
+                out=x_codes[m][:].rearrange("p g r -> p (g r)").bitcast(FP8X4),
+                scales=x_scales[m][:].rearrange("p g r -> p (g r)"),
+                in_=grouped[:].rearrange("p g r t -> p (g r t)"),
+            )
+
+        def mx_product(codes, scales, chunk_tile, planes, j):
+            acc = sums.tile([P, CHUNK], F32, tag="sum")
+            for g in range(GROUPS_K):
+                nc.tensor.matmul_mx(
+                    out=acc[:],
+                    lhsT=codes[:, g, :].bitcast(FP8X4),
+                    lhsT_scale=scales[:, g, :],
+                    rhs=chunk_tile[:, g, :].bitcast(FP8X4),
+                    rhs_scale=planes[4 * g : P, CHUNK * j : CHUNK * (j + 1)],
+                    start=(g == 0),
+                    stop=(g == GROUPS_K - 1),
+                )
+            return acc
+
+        h_sorted = {}
+
+        def layer1(m, j):
+            acc = mx_product(x_codes[m], x_scales[m], w_chunks[j], w_planes, j)
+            if j % 2 == 0:
+                h_sorted[(m, j // 2)] = stage.tile([P, 2, PACK, P], BF16, name="h_sorted", tag="h_sorted")
+            nc.vector.tensor_tensor(
+                out=h_sorted[(m, j // 2)][:, j % 2, :, :],
+                in0=acc[:].rearrange("p (q t) -> p t q", t=PACK),
+                in1=b_sorted[:, j, :, :],
+                op=ALU.add,
+            )
+
+        def turn_h(m, pair):
+            bank = turned.tile([P, 2, PACK, P], BF16, tag="turned")
+            for j2 in range(2):
+                for t in range(PACK):
+                    nc.tensor.transpose(bank[:, j2, t, :], h_sorted[(m, pair)][:, j2, t, :], ident_bf16[:])
+            grouped = stage.tile([P, 2, P, PACK], BF16, align_bytes=64, tag="h_grouped")
+            nc.scalar.copy(out=grouped[:], in_=bank[:].rearrange("p j t r -> p j r t"))
+            return grouped
+
+        def quantise_h(m, pair, grouped):
+            nc.vector.quantize_mx(
+                out=h_codes[m][:, 2 * pair : 2 * pair + 2, :].rearrange("p g r -> p (g r)").bitcast(FP8X4),
+                scales=h_scales[m][:, 2 * pair : 2 * pair + 2, :].rearrange("p g r -> p (g r)"),
+                in_=grouped[:].rearrange("p j r t -> p (j r t)"),
+            )
+
+        def layer2(tiles, j):
+            cols = slice(CHUNK * j, CHUNK * (j + 1))
+            acc, turns, whole, frac, cosine, size, keep_sign, result = {}, {}, {}, {}, {}, {}, {}, {}
+            for m in tiles:
+                acc[m] = mx_product(h_codes[m], h_scales[m], g_chunks[j], g_planes, j)
+            for m in tiles:
+                turns[m] = tail.tile([P, CHUNK], F32, name="turns", tag="turns")
+                nc.vector.scalar_tensor_tensor(
+                    out=turns[m][:], in0=acc[m][:], scalar=1.0 / (2.0 * math.pi), in1=g_turns[:, cols],
+                    op0=ALU.mult, op1=ALU.add,
+                )
+            for m in tiles:
+                whole[m] = tail.tile([P, CHUNK], I32, name="whole", tag="whole")
+                nc.vector.tensor_copy(out=whole[m][:], in_=turns[m][:])
+            for m in tiles:
+                frac[m] = tail.tile([P, CHUNK], F32, name="frac", tag="frac")
+                nc.vector.tensor_tensor(out=frac[m][:], in0=turns[m][:], in1=whole[m][:], op=ALU.subtract)
+            for m in tiles:
+                cosine[m] = tail.tile([P, CHUNK], F32, name="cosine", tag="cosine")
+                nc.scalar.activation(out=cosine[m][:], in_=frac[m][:], func=ACT.Sin, scale=2.0 * math.pi)
+            for m in tiles:
+                size[m] = tail.tile([P, CHUNK], F32, name="size", tag="size")
+                nc.scalar.activation(out=size[m][:], in_=cosine[m][:], func=ACT.Abs)
+            for m in tiles:
+                keep_sign[m] = tail.tile([P, CHUNK], F32, name="keep_sign", tag="keep_sign")
+                nc.scalar.activation(out=keep_sign[m][:], in_=size[m][:], func=ACT.Sign, bias=neg_eps[:])
+            for m in tiles:
+                result[m] = tail.tile([P, CHUNK], F32, name="result", tag="result")
+                nc.gpsimd.tensor_tensor(out=result[m][:], in0=cosine[m][:], in1=keep_sign[m][:], op=ALU.mult)
+                nc.sync.dma_start(out=out[P * m : P * (m + 1), cols], in_=result[m][:])
+
+        for j in range(CHUNKS):
+            spread = spread_chunk(b_rows, j)
+            nc.scalar.copy(out=b_sorted[:, j, :, :], in_=spread[:].rearrange("p (q t) -> p t q", t=PACK))
+        x_grouped = {}
+        for m in TILE_SETS[0]:
+            x_grouped[m] = turn_x(m)
+        for m in TILE_SETS[0]:
+            quantise_x(m, x_grouped[m])
+        for j in range(CHUNKS):
+            spread = spread_chunk(g_bias_rows, j)
+            nc.scalar.activation(
+                out=g_turns[:, CHUNK * j : CHUNK * (j + 1)], in_=spread[:], func=ACT.Copy,
+                scale=1.0 / (2.0 * math.pi), bias=0.25,
+            )
+
+        for s, tiles in enumerate(TILE_SETS):
+            before = TILE_SETS[s - 1] if s > 0 else ()
+            after = TILE_SETS[s + 1] if s + 1 < len(TILE_SETS) else ()
+            h_grouped = {}
+            for step in range(CHUNKS):
+                if step < CHUNKS - 1 and before:
+                    layer2(before, step)
+                for m in tiles:
+                    layer1(m, step)
+                if step == 3:
+                    for m in tiles:
+                        quantise_h(m, 0, h_grouped[m])
+                if step >= 2:
+                    for m in tiles:
+                        h_grouped[m] = turn_h(m, step - 2)
+            if before:
+                layer2(before, CHUNKS - 1)
+            for m in tiles:
+                quantise_h(m, 1, h_grouped[m])
+            for m in after:
+                x_grouped[m] = turn_x(m)
+            for m in after:
+                quantise_x(m, x_grouped[m])
+        for j in range(CHUNKS):
+            layer2(TILE_SETS[-1], j)

@@ -21,11 +21,12 @@ K_PASS = P * PACK
 CHUNK = 512
 BATCH, D = 512, 2048
 TILES = BATCH // P
-GROUPS_K = D // K_PASS
+GROUPS = D // K_PASS
 CHUNKS = D // CHUNK
 EPS = 0.01
+TURN = 2.0 * math.pi
 
-TILE_SETS = ((0, 1), (2, 3))
+FIRST, SECOND = (0, 1), (2, 3)
 
 
 def tile_onehiddenlayer_kernel(tc, x, W_words, W_scales, b, g_words, g_scales, g_bias, out):
@@ -38,10 +39,10 @@ def tile_onehiddenlayer_kernel(tc, x, W_words, W_scales, b, g_words, g_scales, g
         sums = ctx.enter_context(tc.psum_pool(name="sums", bufs=4))
         turned = ctx.enter_context(tc.psum_pool(name="turned", bufs=4))
 
-        w_planes = keep.tile([P, D], U8, align_bytes=64)
-        g_planes = keep.tile([P, D], U8, align_bytes=64)
         b_rows = keep.tile([P, D], BF16)
         g_bias_rows = keep.tile([P, D], BF16)
+        w_planes = keep.tile([P, D], U8, align_bytes=64)
+        g_planes = keep.tile([P, D], U8, align_bytes=64)
         zero_col = keep.tile([P, 1], F32)
         sin_col = keep.tile([P, 1], F32)
         neg_eps = keep.tile([P, 1], F32)
@@ -51,12 +52,12 @@ def tile_onehiddenlayer_kernel(tc, x, W_words, W_scales, b, g_words, g_scales, g
         b_sorted = keep.tile([P, CHUNKS, PACK, P], F32)
         g_turns = keep.tile([P, D], F32)
         x_rows = [keep.tile([P, D], BF16, name="x_rows%d" % m) for m in range(TILES)]
-        w_chunks = [keep.tile([P, GROUPS_K, CHUNK], U32, name="w_chunk%d" % j, align_bytes=64) for j in range(CHUNKS)]
-        g_chunks = [keep.tile([P, GROUPS_K, CHUNK], U32, name="g_chunk%d" % j, align_bytes=64) for j in range(CHUNKS)]
-        x_codes = [keep.tile([P, GROUPS_K, P], U32, name="x_codes%d" % m, align_bytes=64) for m in range(TILES)]
-        x_scales = [keep.tile([P, GROUPS_K, P], U8, name="x_scales%d" % m, align_bytes=64) for m in range(TILES)]
-        h_codes = [keep.tile([P, GROUPS_K, P], U32, name="h_codes%d" % m, align_bytes=64) for m in range(TILES)]
-        h_scales = [keep.tile([P, GROUPS_K, P], U8, name="h_scales%d" % m, align_bytes=64) for m in range(TILES)]
+        w_chunks = [keep.tile([P, GROUPS, CHUNK], U32, name="w_chunk%d" % j, align_bytes=64) for j in range(CHUNKS)]
+        g_chunks = [keep.tile([P, GROUPS, CHUNK], U32, name="g_chunk%d" % j, align_bytes=64) for j in range(CHUNKS)]
+        x_codes = [keep.tile([P, GROUPS, P], U32, name="x_codes%d" % m, align_bytes=64) for m in range(TILES)]
+        x_scales = [keep.tile([P, GROUPS, P], U8, name="x_scales%d" % m, align_bytes=64) for m in range(TILES)]
+        h_codes = [keep.tile([P, GROUPS, P], U32, name="h_codes%d" % m, align_bytes=64) for m in range(TILES)]
+        h_scales = [keep.tile([P, GROUPS, P], U8, name="h_scales%d" % m, align_bytes=64) for m in range(TILES)]
 
         nc.vector.memset(b_rows[:].bitcast(I32), 0)
         nc.vector.memset(w_planes[:].bitcast(I32), 0)
@@ -88,15 +89,14 @@ def tile_onehiddenlayer_kernel(tc, x, W_words, W_scales, b, g_words, g_scales, g
         nc.scalar.dma_start(out=b_rows[0:1, :], in_=b.unsqueeze(0))
         nc.scalar.dma_start(out=g_bias_rows[0:1, :], in_=g_bias.unsqueeze(0))
         load_planes(w_planes, W_scales)
-        for m in TILE_SETS[0]:
+        for m in FIRST:
             load_x(m)
         for j in range(CHUNKS):
             load_chunk(w_chunks[j], W_words, j)
-        load_x(TILE_SETS[1][0])
+        for m in SECOND:
+            load_x(m)
         load_planes(g_planes, g_scales)
-        load_chunk(g_chunks[0], g_words, 0)
-        load_x(TILE_SETS[1][1])
-        for j in range(1, CHUNKS):
+        for j in range(CHUNKS):
             load_chunk(g_chunks[j], g_words, j)
 
         nc.scalar.activation(out=sin_col[:], in_=zero_col[:], func=ACT.Sin)
@@ -106,21 +106,17 @@ def tile_onehiddenlayer_kernel(tc, x, W_words, W_scales, b, g_words, g_scales, g
             nc.tensor.matmul(out=spread[:], lhsT=ones[:], rhs=rows[:, CHUNK * j : CHUNK * (j + 1)], start=True, stop=True)
             return spread
 
-        def turn_x(m):
+        def turn_x(m, second_copy):
             words = x_rows[m][:].bitcast(F32)
-            grouped = stage.tile([P, GROUPS_K, P, PACK], BF16, align_bytes=64, tag="x_grouped")
+            grouped = stage.tile([P, GROUPS, P, PACK], BF16, align_bytes=64, tag="x_grouped")
             for half in range(2):
                 bank = turned.tile([P, 2, 2, P], F32, tag="turned")
                 for g2 in range(2):
                     g = 2 * half + g2
                     for u in range(2):
                         nc.tensor.transpose(bank[:, g2, u, :], words[:, 256 * g + u : 256 * (g + 1) : 2], ident_f32[:])
-                dst = grouped[:].bitcast(F32)[:, 2 * half : 2 * half + 2, :, :]
-                src = bank[:].rearrange("p g u r -> p g r u")
-                if half == 0:
-                    nc.scalar.copy(out=dst, in_=src)
-                else:
-                    nc.vector.tensor_copy(out=dst, in_=src)
+                copy = nc.scalar.copy if half == 0 else second_copy
+                copy(out=grouped[:].bitcast(F32)[:, 2 * half : 2 * half + 2, :, :], in_=bank[:].rearrange("p g u r -> p g r u"))
             return grouped
 
         def quantise_x(m, grouped):
@@ -132,7 +128,7 @@ def tile_onehiddenlayer_kernel(tc, x, W_words, W_scales, b, g_words, g_scales, g
 
         def mx_product(codes, scales, chunk_tile, planes, j):
             acc = sums.tile([P, CHUNK], F32, tag="sum")
-            for g in range(GROUPS_K):
+            for g in range(GROUPS):
                 nc.tensor.matmul_mx(
                     out=acc[:],
                     lhsT=codes[:, g, :].bitcast(FP8X4),
@@ -140,107 +136,117 @@ def tile_onehiddenlayer_kernel(tc, x, W_words, W_scales, b, g_words, g_scales, g
                     rhs=chunk_tile[:, g, :].bitcast(FP8X4),
                     rhs_scale=planes[4 * g : P, CHUNK * j : CHUNK * (j + 1)],
                     start=(g == 0),
-                    stop=(g == GROUPS_K - 1),
+                    stop=(g == GROUPS - 1),
                 )
             return acc
 
-        h_sorted = {}
+        h_sorted, h_grouped, x_grouped = {}, {}, {}
 
-        def layer1(m, j):
-            acc = mx_product(x_codes[m], x_scales[m], w_chunks[j], w_planes, j)
-            if j % 2 == 0:
-                h_sorted[(m, j // 2)] = stage.tile([P, 2, PACK, P], BF16, name="h_sorted", tag="h_sorted")
-            nc.vector.tensor_tensor(
-                out=h_sorted[(m, j // 2)][:, j % 2, :, :],
-                in0=acc[:].rearrange("p (q t) -> p t q", t=PACK),
-                in1=b_sorted[:, j, :, :],
-                op=ALU.add,
-            )
-
-        def turn_h(m, pair):
-            bank = turned.tile([P, 2, PACK, P], BF16, tag="turned")
-            for j2 in range(2):
-                for t in range(PACK):
-                    nc.tensor.transpose(bank[:, j2, t, :], h_sorted[(m, pair)][:, j2, t, :], ident_bf16[:])
-            grouped = stage.tile([P, 2, P, PACK], BF16, align_bytes=64, tag="h_grouped")
-            nc.scalar.copy(out=grouped[:], in_=bank[:].rearrange("p j t r -> p j r t"))
-            return grouped
-
-        def quantise_h(m, pair, grouped):
-            nc.vector.quantize_mx(
-                out=h_codes[m][:, 2 * pair : 2 * pair + 2, :].rearrange("p g r -> p (g r)").bitcast(FP8X4),
-                scales=h_scales[m][:, 2 * pair : 2 * pair + 2, :].rearrange("p g r -> p (g r)"),
-                in_=grouped[:].rearrange("p j r t -> p (j r t)"),
-            )
-
-        def layer2(tiles, j):
-            cols = slice(CHUNK * j, CHUNK * (j + 1))
-            acc, turns, whole, frac, cosine, size, keep_sign, result = {}, {}, {}, {}, {}, {}, {}, {}
+        def layer1(tiles, j):
             for m in tiles:
-                acc[m] = mx_product(h_codes[m], h_scales[m], g_chunks[j], g_planes, j)
-            for m in tiles:
-                turns[m] = tail.tile([P, CHUNK], F32, name="turns", tag="turns")
-                nc.vector.scalar_tensor_tensor(
-                    out=turns[m][:], in0=acc[m][:], scalar=1.0 / (2.0 * math.pi), in1=g_turns[:, cols],
-                    op0=ALU.mult, op1=ALU.add,
+                acc = mx_product(x_codes[m], x_scales[m], w_chunks[j], w_planes, j)
+                if j % 2 == 0:
+                    h_sorted[(m, j // 2)] = stage.tile([P, 2, PACK, P], BF16, name="h_sorted", tag="h_sorted")
+                nc.vector.tensor_tensor(
+                    out=h_sorted[(m, j // 2)][:, j % 2, :, :],
+                    in0=acc[:].rearrange("p (q t) -> p t q", t=PACK),
+                    in1=b_sorted[:, j, :, :],
+                    op=ALU.add,
                 )
+
+        def turn_h(tiles, pair, second_copy):
             for m in tiles:
-                whole[m] = tail.tile([P, CHUNK], I32, name="whole", tag="whole")
-                nc.vector.tensor_copy(out=whole[m][:], in_=turns[m][:])
+                bank = turned.tile([P, 2, PACK, P], BF16, tag="turned")
+                for j2 in range(2):
+                    for t in range(PACK):
+                        nc.tensor.transpose(bank[:, j2, t, :], h_sorted[(m, pair)][:, j2, t, :], ident_bf16[:])
+                h_grouped[(m, pair)] = stage.tile([P, 2, P, PACK], BF16, align_bytes=64, name="h_grouped", tag="h_grouped")
+                copy = nc.scalar.copy if m == tiles[0] else second_copy
+                copy(out=h_grouped[(m, pair)][:], in_=bank[:].rearrange("p j t r -> p j r t"))
+
+        def quantise_h(tiles, pair):
             for m in tiles:
-                frac[m] = tail.tile([P, CHUNK], F32, name="frac", tag="frac")
-                nc.vector.tensor_tensor(out=frac[m][:], in0=turns[m][:], in1=whole[m][:], op=ALU.subtract)
-            for m in tiles:
-                cosine[m] = tail.tile([P, CHUNK], F32, name="cosine", tag="cosine")
-                nc.scalar.activation(out=cosine[m][:], in_=frac[m][:], func=ACT.Sin, scale=2.0 * math.pi)
-            for m in tiles:
-                size[m] = tail.tile([P, CHUNK], F32, name="size", tag="size")
-                nc.scalar.activation(out=size[m][:], in_=cosine[m][:], func=ACT.Abs)
-            for m in tiles:
-                keep_sign[m] = tail.tile([P, CHUNK], F32, name="keep_sign", tag="keep_sign")
-                nc.scalar.activation(out=keep_sign[m][:], in_=size[m][:], func=ACT.Sign, bias=neg_eps[:])
-            for m in tiles:
-                result[m] = tail.tile([P, CHUNK], F32, name="result", tag="result")
-                nc.gpsimd.tensor_tensor(out=result[m][:], in0=cosine[m][:], in1=keep_sign[m][:], op=ALU.mult)
-                nc.sync.dma_start(out=out[P * m : P * (m + 1), cols], in_=result[m][:])
+                nc.vector.quantize_mx(
+                    out=h_codes[m][:, 2 * pair : 2 * pair + 2, :].rearrange("p g r -> p (g r)").bitcast(FP8X4),
+                    scales=h_scales[m][:, 2 * pair : 2 * pair + 2, :].rearrange("p g r -> p (g r)"),
+                    in_=h_grouped[(m, pair)][:].rearrange("p j r t -> p (j r t)"),
+                )
+
+        def layer2_products(tiles, j):
+            return [mx_product(h_codes[m], h_scales[m], g_chunks[j], g_planes, j) for m in tiles]
+
+        def layer2_tail(tiles, j, accs, product):
+            cols = slice(CHUNK * j, CHUNK * (j + 1))
+            both = range(len(tiles))
+            turns = [tail.tile([P, CHUNK], F32, name="turns", tag="turns") for i in both]
+            whole = [tail.tile([P, CHUNK], I32, name="whole", tag="whole") for i in both]
+            frac = [tail.tile([P, CHUNK], F32, name="frac", tag="frac") for i in both]
+            cosine = [tail.tile([P, CHUNK], F32, name="cosine", tag="cosine") for i in both]
+            size = [tail.tile([P, CHUNK], F32, name="size", tag="size") for i in both]
+            keep_sign = [tail.tile([P, CHUNK], F32, name="keep_sign", tag="keep_sign") for i in both]
+            result = [tail.tile([P, CHUNK], F32, name="result", tag="result") for i in both]
+            for i in both:
+                nc.vector.scalar_tensor_tensor(
+                    out=turns[i][:], in0=accs[i][:], scalar=1.0 / TURN, in1=g_turns[:, cols], op0=ALU.mult, op1=ALU.add
+                )
+            for i in both:
+                nc.vector.tensor_copy(out=whole[i][:], in_=turns[i][:])
+            for i in both:
+                nc.vector.tensor_tensor(out=frac[i][:], in0=turns[i][:], in1=whole[i][:], op=ALU.subtract)
+            for i in both:
+                nc.scalar.activation(out=cosine[i][:], in_=frac[i][:], func=ACT.Sin, scale=TURN)
+            for i in both:
+                nc.scalar.activation(out=size[i][:], in_=cosine[i][:], func=ACT.Abs)
+            for i in both:
+                nc.scalar.activation(out=keep_sign[i][:], in_=size[i][:], func=ACT.Sign, bias=neg_eps[:])
+            for i in both:
+                product(out=result[i][:], in0=cosine[i][:], in1=keep_sign[i][:], op=ALU.mult)
+                nc.sync.dma_start(out=out[P * tiles[i] : P * (tiles[i] + 1), cols], in_=result[i][:])
+
+        def layer2(tiles, j, product):
+            layer2_tail(tiles, j, layer2_products(tiles, j), product)
 
         for j in range(CHUNKS):
             spread = spread_chunk(b_rows, j)
             nc.scalar.copy(out=b_sorted[:, j, :, :], in_=spread[:].rearrange("p (q t) -> p t q", t=PACK))
-        x_grouped = {}
-        for m in TILE_SETS[0]:
-            x_grouped[m] = turn_x(m)
-        for m in TILE_SETS[0]:
+        for m in FIRST:
+            x_grouped[m] = turn_x(m, nc.vector.tensor_copy)
+        for m in FIRST:
             quantise_x(m, x_grouped[m])
         for j in range(CHUNKS):
             spread = spread_chunk(g_bias_rows, j)
             nc.scalar.activation(
-                out=g_turns[:, CHUNK * j : CHUNK * (j + 1)], in_=spread[:], func=ACT.Copy,
-                scale=1.0 / (2.0 * math.pi), bias=0.25,
+                out=g_turns[:, CHUNK * j : CHUNK * (j + 1)], in_=spread[:], func=ACT.Copy, scale=1.0 / TURN, bias=0.25
             )
 
-        for s, tiles in enumerate(TILE_SETS):
-            before = TILE_SETS[s - 1] if s > 0 else ()
-            after = TILE_SETS[s + 1] if s + 1 < len(TILE_SETS) else ()
-            h_grouped = {}
-            for step in range(CHUNKS):
-                if step < CHUNKS - 1 and before:
-                    layer2(before, step)
-                for m in tiles:
-                    layer1(m, step)
-                if step == 3:
-                    for m in tiles:
-                        quantise_h(m, 0, h_grouped[m])
-                if step >= 2:
-                    for m in tiles:
-                        h_grouped[m] = turn_h(m, step - 2)
-            if before:
-                layer2(before, CHUNKS - 1)
-            for m in tiles:
-                quantise_h(m, 1, h_grouped[m])
-            for m in after:
-                x_grouped[m] = turn_x(m)
-            for m in after:
-                quantise_x(m, x_grouped[m])
-        for j in range(CHUNKS):
-            layer2(TILE_SETS[-1], j)
+        layer1(FIRST, 0)
+        layer1(FIRST, 1)
+        layer1(FIRST, 2)
+        turn_h(FIRST, 0, nc.scalar.copy)
+        layer1(FIRST, 3)
+        quantise_h(FIRST, 0)
+        turn_h(FIRST, 1, nc.vector.tensor_copy)
+        quantise_h(FIRST, 1)
+        for m in SECOND:
+            x_grouped[m] = turn_x(m, nc.scalar.copy)
+        for m in SECOND:
+            quantise_x(m, x_grouped[m])
+
+        layer2(FIRST, 0, nc.gpsimd.tensor_tensor)
+        layer1(SECOND, 0)
+        layer2(FIRST, 1, nc.gpsimd.tensor_tensor)
+        layer1(SECOND, 1)
+        accs = layer2_products(FIRST, 2)
+        turn_h(SECOND, 0, nc.scalar.copy)
+        layer2_tail(FIRST, 2, accs, nc.gpsimd.tensor_tensor)
+        layer1(SECOND, 2)
+        quantise_h(SECOND, 0)
+        layer1(SECOND, 3)
+        turn_h(SECOND, 1, nc.vector.tensor_copy)
+        accs = layer2_products(FIRST, 3)
+        quantise_h(SECOND, 1)
+        layer2_tail(FIRST, 3, accs, nc.gpsimd.tensor_tensor)
+
+        for j in range(CHUNKS - 1):
+            layer2(SECOND, j, nc.gpsimd.tensor_tensor)
+        layer2(SECOND, CHUNKS - 1, nc.vector.tensor_tensor)

@@ -49,7 +49,7 @@ def tile_onehiddenlayer_kernel(tc, x, W_words, W_scales, b, g_words, g_scales, g
         ones = keep.tile([P, P], BF16)
         ident_f32 = keep.tile([P, P], F32)
         ident_bf16 = keep.tile([P, P], BF16)
-        b_sorted = keep.tile([P, CHUNKS, PACK, P], F32)
+        b_sorted = keep.tile([P, CHUNKS, 2, P, 2], F32)
         g_turns = keep.tile([P, D], F32)
         x_rows = [keep.tile([P, D], BF16, name="x_rows%d" % m) for m in range(TILES)]
         w_chunks = [keep.tile([P, GROUPS, CHUNK], U32, name="w_chunk%d" % j, align_bytes=64) for j in range(CHUNKS)]
@@ -148,9 +148,9 @@ def tile_onehiddenlayer_kernel(tc, x, W_words, W_scales, b, g_words, g_scales, g
                 if j % 2 == 0:
                     h_sorted[(m, j // 2)] = stage.tile([P, 2, PACK, P], BF16, name="h_sorted", tag="h_sorted")
                 nc.vector.tensor_tensor(
-                    out=h_sorted[(m, j // 2)][:, j % 2, :, :],
-                    in0=acc[:].rearrange("p (q t) -> p t q", t=PACK),
-                    in1=b_sorted[:, j, :, :],
+                    out=h_sorted[(m, j // 2)][:, j % 2, :, :].rearrange("p (u e) q -> p u q e", e=2),
+                    in0=acc[:].rearrange("p (q u e) -> p u q e", u=2, e=2),
+                    in1=b_sorted[:, j, :, :, :],
                     op=ALU.add,
                 )
 
@@ -208,7 +208,7 @@ def tile_onehiddenlayer_kernel(tc, x, W_words, W_scales, b, g_words, g_scales, g
 
         for j in range(CHUNKS):
             spread = spread_chunk(b_rows, j)
-            nc.scalar.copy(out=b_sorted[:, j, :, :], in_=spread[:].rearrange("p (q t) -> p t q", t=PACK))
+            nc.scalar.copy(out=b_sorted[:, j, :, :, :], in_=spread[:].rearrange("p (q u e) -> p u q e", u=2, e=2))
         for m in FIRST:
             x_grouped[m] = turn_x(m, nc.vector.tensor_copy)
         for m in FIRST:

@@ -27,6 +27,8 @@ EPS = 0.01
 TURN = 2.0 * math.pi
 
 FIRST, SECOND = (0, 1), (2, 3)
+LAST_ON_GPSIMD = 14
+LAYER2_ORDER = [(m, j) for j in range(CHUNKS) for m in FIRST] + [(m, j) for m in SECOND for j in range(CHUNKS)]
 
 
 def tile_onehiddenlayer_kernel(tc, x, W_words, W_scales, b, g_words, g_scales, g_bias, out):
@@ -39,14 +41,13 @@ def tile_onehiddenlayer_kernel(tc, x, W_words, W_scales, b, g_words, g_scales, g
         sums = ctx.enter_context(tc.psum_pool(name="sums", bufs=4))
         turned = ctx.enter_context(tc.psum_pool(name="turned", bufs=4))
 
-        b_rows = keep.tile([P, D], BF16)
-        g_bias_rows = keep.tile([P, D], BF16)
+        bias_rows = keep.tile([P, CHUNK], BF16)
+        idle = keep.tile([P, CHUNK], BF16)
         w_planes = keep.tile([P, D], U8, align_bytes=64)
         g_planes = keep.tile([P, D], U8, align_bytes=64)
         zero_col = keep.tile([P, 1], F32)
         sin_col = keep.tile([P, 1], F32)
         neg_eps = keep.tile([P, 1], F32)
-        ones = keep.tile([P, P], BF16)
         ident_f32 = keep.tile([P, P], F32)
         ident_bf16 = keep.tile([P, P], BF16)
         b_sorted = keep.tile([P, CHUNKS, 2, P, 2], F32)
@@ -59,15 +60,14 @@ def tile_onehiddenlayer_kernel(tc, x, W_words, W_scales, b, g_words, g_scales, g
         h_codes = [keep.tile([P, GROUPS, P], U32, name="h_codes%d" % m, align_bytes=64) for m in range(TILES)]
         h_scales = [keep.tile([P, GROUPS, P], U8, name="h_scales%d" % m, align_bytes=64) for m in range(TILES)]
 
-        nc.vector.memset(b_rows[:].bitcast(I32), 0)
-        nc.vector.memset(w_planes[:].bitcast(I32), 0)
-        nc.vector.memset(g_bias_rows[:].bitcast(I32), 0)
-        nc.vector.memset(g_planes[:].bitcast(I32), 0)
         nc.vector.memset(zero_col[:], 0.0)
-        nc.vector.memset(neg_eps[:], -EPS)
-        nc.gpsimd.memset(ones[:], 1.0)
+        nc.vector.memset(idle[:].bitcast(I32), 0)
+        nc.vector.memset(bias_rows[:].bitcast(I32), 0)
+        nc.vector.memset(w_planes[:].bitcast(I32), 0)
         make_identity(nc, ident_f32[:])
-        make_identity(nc, ident_bf16[:])
+        nc.vector.tensor_copy(out=ident_bf16[:], in_=ident_f32[:])
+        nc.vector.memset(neg_eps[:], -EPS)
+        nc.vector.memset(g_planes[:].bitcast(I32), 0)
 
         def load_planes(planes, scales):
             for quadrant in range(4):
@@ -86,25 +86,33 @@ def tile_onehiddenlayer_kernel(tc, x, W_words, W_scales, b, g_words, g_scales, g
         def load_x(m):
             nc.sync.dma_start(out=x_rows[m][:], in_=x[P * m : P * (m + 1), :])
 
-        nc.scalar.dma_start(out=b_rows[0:1, :], in_=b.unsqueeze(0))
-        nc.scalar.dma_start(out=g_bias_rows[0:1, :], in_=g_bias.unsqueeze(0))
+        load_x(FIRST[0])
+        nc.sync.dma_start(out=bias_rows[0:CHUNKS, :], in_=b.rearrange("(j n) -> j n", j=CHUNKS))
+        nc.sync.dma_start(out=bias_rows[CHUNKS : 2 * CHUNKS, :], in_=g_bias.rearrange("(j n) -> j n", j=CHUNKS))
+        load_x(FIRST[1])
         load_planes(w_planes, W_scales)
-        for m in FIRST:
-            load_x(m)
         for j in range(CHUNKS):
             load_chunk(w_chunks[j], W_words, j)
-        for m in SECOND:
-            load_x(m)
         load_planes(g_planes, g_scales)
-        for j in range(CHUNKS):
+        load_chunk(g_chunks[0], g_words, 0)
+        load_x(SECOND[0])
+        load_chunk(g_chunks[1], g_words, 1)
+        load_x(SECOND[1])
+        for j in range(2, CHUNKS):
             load_chunk(g_chunks[j], g_words, j)
 
         nc.scalar.activation(out=sin_col[:], in_=zero_col[:], func=ACT.Sin)
 
-        def spread_chunk(rows, j):
+        def spread_chunk(row):
             spread = sums.tile([P, CHUNK], F32, tag="sum")
-            nc.tensor.matmul(out=spread[:], lhsT=ones[:], rhs=rows[:, CHUNK * j : CHUNK * (j + 1)], start=True, stop=True)
+            selector = ident_bf16[:, row : row + 1].to_broadcast([P, P])
+            nc.tensor.matmul(out=spread[:], lhsT=selector, rhs=bias_rows[:], start=True, stop=True)
             return spread
+
+        def warm_up(passes):
+            spare = sums.tile([P, CHUNK], F32, tag="sum")
+            for i in range(passes):
+                nc.tensor.matmul(out=spare[:], lhsT=idle[:, 0:P], rhs=idle[:], start=True, stop=True)
 
         def turn_x(m, second_copy):
             words = x_rows[m][:].bitcast(F32)
@@ -142,111 +150,189 @@ def tile_onehiddenlayer_kernel(tc, x, W_words, W_scales, b, g_words, g_scales, g
 
         h_sorted, h_grouped, x_grouped = {}, {}, {}
 
-        def layer1(tiles, j):
-            for m in tiles:
-                acc = mx_product(x_codes[m], x_scales[m], w_chunks[j], w_planes, j)
-                if j % 2 == 0:
-                    h_sorted[(m, j // 2)] = stage.tile([P, 2, PACK, P], BF16, name="h_sorted", tag="h_sorted")
-                nc.vector.tensor_tensor(
-                    out=h_sorted[(m, j // 2)][:, j % 2, :, :].rearrange("p (u e) q -> p u q e", e=2),
-                    in0=acc[:].rearrange("p (q u e) -> p u q e", u=2, e=2),
-                    in1=b_sorted[:, j, :, :, :],
-                    op=ALU.add,
-                )
+        layer1_sums = {}
 
-        def turn_h(tiles, pair, second_copy):
-            for m in tiles:
-                bank = turned.tile([P, 2, PACK, P], BF16, tag="turned")
-                for j2 in range(2):
-                    for t in range(PACK):
-                        nc.tensor.transpose(bank[:, j2, t, :], h_sorted[(m, pair)][:, j2, t, :], ident_bf16[:])
-                h_grouped[(m, pair)] = stage.tile([P, 2, P, PACK], BF16, align_bytes=64, name="h_grouped", tag="h_grouped")
-                copy = nc.scalar.copy if m == tiles[0] else second_copy
-                copy(out=h_grouped[(m, pair)][:], in_=bank[:].rearrange("p j t r -> p j r t"))
+        def layer1_product(m, j):
+            layer1_sums[(m, j)] = mx_product(x_codes[m], x_scales[m], w_chunks[j], w_planes, j)
 
-        def quantise_h(tiles, pair):
-            for m in tiles:
-                nc.vector.quantize_mx(
-                    out=h_codes[m][:, 2 * pair : 2 * pair + 2, :].rearrange("p g r -> p (g r)").bitcast(FP8X4),
-                    scales=h_scales[m][:, 2 * pair : 2 * pair + 2, :].rearrange("p g r -> p (g r)"),
-                    in_=h_grouped[(m, pair)][:].rearrange("p j r t -> p (j r t)"),
-                )
+        def layer1_add(m, j):
+            acc = layer1_sums[(m, j)]
+            if j % 2 == 0:
+                h_sorted[(m, j // 2)] = stage.tile([P, 2, 2, P, 2], BF16, name="h_sorted", tag="h_sorted")
+            nc.vector.tensor_tensor(
+                out=h_sorted[(m, j // 2)][:, j % 2, :, :, :],
+                in0=acc[:].rearrange("p (q u e) -> p u q e", u=2, e=2),
+                in1=b_sorted[:, j, :, :, :],
+                op=ALU.add,
+            )
 
-        def layer2_products(tiles, j):
-            return [mx_product(h_codes[m], h_scales[m], g_chunks[j], g_planes, j) for m in tiles]
+        def layer1(m, j):
+            layer1_product(m, j)
+            layer1_add(m, j)
 
-        def layer2_tail(tiles, j, accs, product):
-            cols = slice(CHUNK * j, CHUNK * (j + 1))
-            both = range(len(tiles))
-            turns = [tail.tile([P, CHUNK], F32, name="turns", tag="turns") for i in both]
-            whole = [tail.tile([P, CHUNK], I32, name="whole", tag="whole") for i in both]
-            frac = [tail.tile([P, CHUNK], F32, name="frac", tag="frac") for i in both]
-            cosine = [tail.tile([P, CHUNK], F32, name="cosine", tag="cosine") for i in both]
-            size = [tail.tile([P, CHUNK], F32, name="size", tag="size") for i in both]
-            keep_sign = [tail.tile([P, CHUNK], F32, name="keep_sign", tag="keep_sign") for i in both]
-            result = [tail.tile([P, CHUNK], F32, name="result", tag="result") for i in both]
-            for i in both:
-                nc.vector.scalar_tensor_tensor(
-                    out=turns[i][:], in0=accs[i][:], scalar=1.0 / TURN, in1=g_turns[:, cols], op0=ALU.mult, op1=ALU.add
-                )
-            for i in both:
-                nc.vector.tensor_copy(out=whole[i][:], in_=turns[i][:])
-            for i in both:
-                nc.vector.tensor_tensor(out=frac[i][:], in0=turns[i][:], in1=whole[i][:], op=ALU.subtract)
-            for i in both:
-                nc.scalar.activation(out=cosine[i][:], in_=frac[i][:], func=ACT.Sin, scale=TURN)
-            for i in both:
-                nc.scalar.activation(out=size[i][:], in_=cosine[i][:], func=ACT.Abs)
-            for i in both:
-                nc.scalar.activation(out=keep_sign[i][:], in_=size[i][:], func=ACT.Sign, bias=neg_eps[:])
-            for i in both:
-                product(out=result[i][:], in0=cosine[i][:], in1=keep_sign[i][:], op=ALU.mult)
-                nc.sync.dma_start(out=out[P * tiles[i] : P * (tiles[i] + 1), cols], in_=result[i][:])
+        def turn_h(m, pair, copy):
+            words = h_sorted[(m, pair)][:].rearrange("p j u q e -> p (j u q e)").bitcast(F32)
+            bank = turned.tile([P, 2, 2, P], F32, tag="turned")
+            for j2 in range(2):
+                for u in range(2):
+                    first = P * (2 * j2 + u)
+                    nc.tensor.transpose(bank[:, j2, u, :], words[:, first : first + P], ident_f32[:])
+            h_grouped[(m, pair)] = stage.tile([P, 2, P, PACK], BF16, align_bytes=64, name="h_grouped", tag="h_grouped")
+            copy(out=h_grouped[(m, pair)][:].bitcast(F32), in_=bank[:].rearrange("p j u r -> p j r u"))
 
-        def layer2(tiles, j, product):
-            layer2_tail(tiles, j, layer2_products(tiles, j), product)
+        def quantise_h(m, pair):
+            nc.vector.quantize_mx(
+                out=h_codes[m][:, 2 * pair : 2 * pair + 2, :].rearrange("p g r -> p (g r)").bitcast(FP8X4),
+                scales=h_scales[m][:, 2 * pair : 2 * pair + 2, :].rearrange("p g r -> p (g r)"),
+                in_=h_grouped[(m, pair)][:].rearrange("p j r t -> p (j r t)"),
+            )
 
-        for j in range(CHUNKS):
-            spread = spread_chunk(b_rows, j)
-            nc.scalar.copy(out=b_sorted[:, j, :, :, :], in_=spread[:].rearrange("p (q u e) -> p u q e", u=2, e=2))
+        def spread_g_bias(j):
+            spread = spread_chunk(CHUNKS + j)
+            nc.scalar.activation(
+                out=g_turns[:, CHUNK * j : CHUNK * (j + 1)], in_=spread[:], func=ACT.Copy, scale=1.0 / TURN, bias=0.25
+            )
+
+        flow = {}
+
+        def product(k):
+            m, j = LAYER2_ORDER[k]
+            flow[k] = {"sum": mx_product(h_codes[m], h_scales[m], g_chunks[j], g_planes, j)}
+
+        def take_turns(k):
+            m, j = LAYER2_ORDER[k]
+            flow[k]["turns"] = tail.tile([P, CHUNK], F32, name="turns", tag="turns")
+            nc.vector.scalar_tensor_tensor(
+                out=flow[k]["turns"][:],
+                in0=flow[k]["sum"][:],
+                scalar=1.0 / TURN,
+                in1=g_turns[:, CHUNK * j : CHUNK * (j + 1)],
+                op0=ALU.mult,
+                op1=ALU.add,
+            )
+
+        def take_whole(k):
+            flow[k]["whole"] = tail.tile([P, CHUNK], I32, name="whole", tag="whole")
+            nc.vector.tensor_copy(out=flow[k]["whole"][:], in_=flow[k]["turns"][:])
+
+        def take_frac(k):
+            flow[k]["frac"] = tail.tile([P, CHUNK], F32, name="frac", tag="frac")
+            nc.vector.tensor_tensor(
+                out=flow[k]["frac"][:], in0=flow[k]["turns"][:], in1=flow[k]["whole"][:], op=ALU.subtract
+            )
+
+        def take_cosine(k):
+            flow[k]["cosine"] = tail.tile([P, CHUNK], F32, name="cosine", tag="cosine")
+            nc.scalar.activation(out=flow[k]["cosine"][:], in_=flow[k]["frac"][:], func=ACT.Sin, scale=TURN)
+
+        def take_size(k):
+            flow[k]["size"] = tail.tile([P, CHUNK], F32, name="size", tag="size")
+            nc.scalar.activation(out=flow[k]["size"][:], in_=flow[k]["cosine"][:], func=ACT.Abs)
+
+        def take_sign(k):
+            flow[k]["sign"] = tail.tile([P, CHUNK], F32, name="keep_sign", tag="keep_sign")
+            nc.scalar.activation(out=flow[k]["sign"][:], in_=flow[k]["size"][:], func=ACT.Sign, bias=neg_eps[:])
+
+        def finish(k, multiply):
+            m, j = LAYER2_ORDER[k]
+            flow[k]["result"] = tail.tile([P, CHUNK], F32, name="result", tag="result")
+            multiply(out=flow[k]["result"][:], in0=flow[k]["cosine"][:], in1=flow[k]["sign"][:], op=ALU.mult)
+            nc.sync.dma_start(out=out[P * m : P * (m + 1), CHUNK * j : CHUNK * (j + 1)], in_=flow[k]["result"][:])
+
+        def step(k):
+            if k in flow:
+                take_turns(k)
+            if 2 <= k <= len(LAYER2_ORDER):
+                take_frac(k - 1)
+            if k in flow:
+                take_whole(k)
+            if 2 <= k <= len(LAYER2_ORDER):
+                take_cosine(k - 1)
+            if 2 <= k <= len(LAYER2_ORDER) + 1:
+                take_sign(k - 2)
+                if k - 2 < LAST_ON_GPSIMD:
+                    finish(k - 2, nc.gpsimd.tensor_tensor)
+                else:
+                    finish(k - 2, nc.vector.tensor_tensor)
+            if 1 <= k <= len(LAYER2_ORDER):
+                take_size(k - 1)
+
+        def pair_step(k, m, j, turn=None, quantise=None):
+            product(k)
+            if turn:
+                turn()
+            layer1_product(m, j)
+            take_turns(k)
+            if quantise:
+                quantise()
+            take_whole(k)
+            layer1_add(m, j)
+            take_frac(k)
+            take_cosine(k)
+            take_sign(k - 1)
+            finish(k - 1, nc.gpsimd.tensor_tensor)
+            take_size(k)
+
+        warm_up(6)
         for m in FIRST:
             x_grouped[m] = turn_x(m, nc.vector.tensor_copy)
         for m in FIRST:
             quantise_x(m, x_grouped[m])
         for j in range(CHUNKS):
-            spread = spread_chunk(g_bias_rows, j)
-            nc.scalar.activation(
-                out=g_turns[:, CHUNK * j : CHUNK * (j + 1)], in_=spread[:], func=ACT.Copy, scale=1.0 / TURN, bias=0.25
-            )
+            spread = spread_chunk(j)
+            nc.scalar.copy(out=b_sorted[:, j, :, :, :], in_=spread[:].rearrange("p (q u e) -> p u q e", u=2, e=2))
 
-        layer1(FIRST, 0)
-        layer1(FIRST, 1)
-        layer1(FIRST, 2)
-        turn_h(FIRST, 0, nc.scalar.copy)
-        layer1(FIRST, 3)
-        quantise_h(FIRST, 0)
-        turn_h(FIRST, 1, nc.vector.tensor_copy)
-        quantise_h(FIRST, 1)
-        for m in SECOND:
-            x_grouped[m] = turn_x(m, nc.scalar.copy)
-        for m in SECOND:
-            quantise_x(m, x_grouped[m])
-
-        layer2(FIRST, 0, nc.gpsimd.tensor_tensor)
-        layer1(SECOND, 0)
-        layer2(FIRST, 1, nc.gpsimd.tensor_tensor)
-        layer1(SECOND, 1)
-        accs = layer2_products(FIRST, 2)
-        turn_h(SECOND, 0, nc.scalar.copy)
-        layer2_tail(FIRST, 2, accs, nc.gpsimd.tensor_tensor)
-        layer1(SECOND, 2)
-        quantise_h(SECOND, 0)
-        layer1(SECOND, 3)
-        turn_h(SECOND, 1, nc.vector.tensor_copy)
-        accs = layer2_products(FIRST, 3)
-        quantise_h(SECOND, 1)
-        layer2_tail(FIRST, 3, accs, nc.gpsimd.tensor_tensor)
-
-        for j in range(CHUNKS - 1):
-            layer2(SECOND, j, nc.gpsimd.tensor_tensor)
-        layer2(SECOND, CHUNKS - 1, nc.vector.tensor_tensor)
+        a, c = FIRST
+        d, e = SECOND
+        on_scalar, on_vector = nc.scalar.copy, nc.vector.tensor_copy
+        layer1(a, 0)
+        layer1(c, 0)
+        spread_g_bias(0)
+        layer1(a, 1)
+        layer1(c, 1)
+        spread_g_bias(1)
+        layer1(a, 2)
+        turn_h(a, 0, on_scalar)
+        layer1(a, 3)
+        spread_g_bias(2)
+        quantise_h(a, 0)
+        layer1(c, 2)
+        turn_h(a, 1, on_scalar)
+        turn_h(c, 0, on_scalar)
+        quantise_h(a, 1)
+        spread_g_bias(3)
+        layer1(c, 3)
+        product(0)
+        turn_h(c, 1, on_scalar)
+        x_grouped[d] = turn_x(d, on_scalar)
+        quantise_h(c, 0)
+        take_turns(0)
+        take_whole(0)
+        quantise_h(c, 1)
+        take_frac(0)
+        take_cosine(0)
+        quantise_x(d, x_grouped[d])
+        take_size(0)
+        x_grouped[e] = turn_x(e, on_scalar)
+        pair_step(1, d, 0)
+        pair_step(2, d, 1, quantise=lambda: quantise_x(e, x_grouped[e]))
+        pair_step(3, d, 2, turn=lambda: turn_h(d, 0, on_scalar))
+        pair_step(4, d, 3, quantise=lambda: quantise_h(d, 0))
+        pair_step(5, e, 0, turn=lambda: turn_h(d, 1, on_scalar))
+        pair_step(6, e, 1, quantise=lambda: quantise_h(d, 1))
+        pair_step(7, e, 2, turn=lambda: turn_h(e, 0, on_scalar))
+        pair_step(8, e, 3, quantise=lambda: quantise_h(e, 0))
+        product(9)
+        turn_h(e, 1, on_scalar)
+        take_turns(9)
+        take_whole(9)
+        take_sign(8)
+        finish(8, nc.gpsimd.tensor_tensor)
+        product(10)
+        step(10)
+        quantise_h(e, 1)
+        for k in range(11, len(LAYER2_ORDER)):
+            product(k)
+            step(k)
+        for k in range(len(LAYER2_ORDER), len(LAYER2_ORDER) + 2):
+            step(k)

@@ -27,7 +27,7 @@ EPS = 0.01
 TURN = 2.0 * math.pi
 
 FIRST, SECOND = (0, 1), (2, 3)
-LAST_ON_GPSIMD = 14
+ON_GPSIMD = range(8)
 LAYER2_ORDER = [(m, j) for j in range(CHUNKS) for m in FIRST] + [(m, j) for m in SECOND for j in range(CHUNKS)]
 
 
@@ -61,8 +61,8 @@ def tile_onehiddenlayer_kernel(tc, x, W_words, W_scales, b, g_words, g_scales, g
         h_scales = [keep.tile([P, GROUPS, P], U8, name="h_scales%d" % m, align_bytes=64) for m in range(TILES)]
 
         nc.vector.memset(zero_col[:], 0.0)
-        nc.vector.memset(idle[:].bitcast(I32), 0)
         nc.vector.memset(bias_rows[:].bitcast(I32), 0)
+        nc.vector.memset(idle[:].bitcast(I32), 0)
         nc.vector.memset(w_planes[:].bitcast(I32), 0)
         make_identity(nc, ident_f32[:])
         nc.vector.tensor_copy(out=ident_bf16[:], in_=ident_f32[:])
@@ -86,9 +86,9 @@ def tile_onehiddenlayer_kernel(tc, x, W_words, W_scales, b, g_words, g_scales, g
         def load_x(m):
             nc.sync.dma_start(out=x_rows[m][:], in_=x[P * m : P * (m + 1), :])
 
+        nc.scalar.dma_start(out=bias_rows[0:CHUNKS, :], in_=b.rearrange("(j n) -> j n", j=CHUNKS))
+        nc.scalar.dma_start(out=bias_rows[CHUNKS : 2 * CHUNKS, :], in_=g_bias.rearrange("(j n) -> j n", j=CHUNKS))
         load_x(FIRST[0])
-        nc.sync.dma_start(out=bias_rows[0:CHUNKS, :], in_=b.rearrange("(j n) -> j n", j=CHUNKS))
-        nc.sync.dma_start(out=bias_rows[CHUNKS : 2 * CHUNKS, :], in_=g_bias.rearrange("(j n) -> j n", j=CHUNKS))
         load_x(FIRST[1])
         load_planes(w_planes, W_scales)
         for j in range(CHUNKS):
@@ -114,16 +114,16 @@ def tile_onehiddenlayer_kernel(tc, x, W_words, W_scales, b, g_words, g_scales, g
             for i in range(passes):
                 nc.tensor.matmul(out=spare[:], lhsT=idle[:, 0:P], rhs=idle[:], start=True, stop=True)
 
-        def turn_x(m, second_copy):
+        def turn_x(m, first_copy, second_copy):
             words = x_rows[m][:].bitcast(F32)
-            grouped = stage.tile([P, GROUPS, P, PACK], BF16, align_bytes=64, tag="x_grouped")
+            grouped = stage.tile([P, GROUPS, P, PACK], BF16, align_bytes=64, tag="x_grouped", bufs=2)
             for half in range(2):
                 bank = turned.tile([P, 2, 2, P], F32, tag="turned")
                 for g2 in range(2):
                     g = 2 * half + g2
                     for u in range(2):
                         nc.tensor.transpose(bank[:, g2, u, :], words[:, 256 * g + u : 256 * (g + 1) : 2], ident_f32[:])
-                copy = nc.scalar.copy if half == 0 else second_copy
+                copy = first_copy if half == 0 else second_copy
                 copy(out=grouped[:].bitcast(F32)[:, 2 * half : 2 * half + 2, :, :], in_=bank[:].rearrange("p g u r -> p g r u"))
             return grouped
 
@@ -222,7 +222,7 @@ def tile_onehiddenlayer_kernel(tc, x, W_words, W_scales, b, g_words, g_scales, g
             )
 
         def take_cosine(k):
-            flow[k]["cosine"] = tail.tile([P, CHUNK], F32, name="cosine", tag="cosine")
+            flow[k]["cosine"] = tail.tile([P, CHUNK], F32, name="cosine", tag="cosine", bufs=8)
             nc.scalar.activation(out=flow[k]["cosine"][:], in_=flow[k]["frac"][:], func=ACT.Sin, scale=TURN)
 
         def take_size(k):
@@ -230,7 +230,7 @@ def tile_onehiddenlayer_kernel(tc, x, W_words, W_scales, b, g_words, g_scales, g
             nc.scalar.activation(out=flow[k]["size"][:], in_=flow[k]["cosine"][:], func=ACT.Abs)
 
         def take_sign(k):
-            flow[k]["sign"] = tail.tile([P, CHUNK], F32, name="keep_sign", tag="keep_sign")
+            flow[k]["sign"] = tail.tile([P, CHUNK], F32, name="keep_sign", tag="keep_sign", bufs=8)
             nc.scalar.activation(out=flow[k]["sign"][:], in_=flow[k]["size"][:], func=ACT.Sign, bias=neg_eps[:])
 
         def finish(k, multiply):
@@ -239,100 +239,110 @@ def tile_onehiddenlayer_kernel(tc, x, W_words, W_scales, b, g_words, g_scales, g
             multiply(out=flow[k]["result"][:], in0=flow[k]["cosine"][:], in1=flow[k]["sign"][:], op=ALU.mult)
             nc.sync.dma_start(out=out[P * m : P * (m + 1), CHUNK * j : CHUNK * (j + 1)], in_=flow[k]["result"][:])
 
-        def step(k):
-            if k in flow:
-                take_turns(k)
-            if 2 <= k <= len(LAYER2_ORDER):
-                take_frac(k - 1)
-            if k in flow:
-                take_whole(k)
-            if 2 <= k <= len(LAYER2_ORDER):
-                take_cosine(k - 1)
-            if 2 <= k <= len(LAYER2_ORDER) + 1:
-                take_sign(k - 2)
-                if k - 2 < LAST_ON_GPSIMD:
-                    finish(k - 2, nc.gpsimd.tensor_tensor)
-                else:
-                    finish(k - 2, nc.vector.tensor_tensor)
-            if 1 <= k <= len(LAYER2_ORDER):
-                take_size(k - 1)
+        def multiply(k):
+            finish(k, nc.gpsimd.tensor_tensor if k in ON_GPSIMD else nc.vector.tensor_tensor)
 
-        def pair_step(k, m, j, turn=None, quantise=None):
+        def single_step(k, other=None, turn=None, quantise=None):
             product(k)
             if turn:
                 turn()
-            layer1_product(m, j)
+            if other:
+                layer1_product(*other)
             take_turns(k)
+            if other:
+                layer1_add(*other)
+            take_whole(k)
             if quantise:
                 quantise()
-            take_whole(k)
-            layer1_add(m, j)
+            if k >= 3 and k - 3 not in ON_GPSIMD:
+                multiply(k - 3)
             take_frac(k)
             take_cosine(k)
-            take_sign(k - 1)
-            finish(k - 1, nc.gpsimd.tensor_tensor)
             take_size(k)
+            if k >= 1:
+                take_sign(k - 1)
+                if k - 1 in ON_GPSIMD:
+                    multiply(k - 1)
 
-        warm_up(6)
-        for m in FIRST:
-            x_grouped[m] = turn_x(m, nc.vector.tensor_copy)
-        for m in FIRST:
-            quantise_x(m, x_grouped[m])
-        for j in range(CHUNKS):
+        def double_step(k, quantise=None):
+            both = (k, k + 1)
+            for i in both:
+                product(i)
+            if quantise:
+                quantise()
+            for i in (k - 6, k - 5):
+                if i not in ON_GPSIMD:
+                    multiply(i)
+            for i in both:
+                take_turns(i)
+            for i in both:
+                take_whole(i)
+            for i in both:
+                take_frac(i)
+            for i in both:
+                take_cosine(i)
+            for i in both:
+                take_size(i)
+            for i in both:
+                take_sign(i)
+        def spread_b(j):
             spread = spread_chunk(j)
             nc.scalar.copy(out=b_sorted[:, j, :, :, :], in_=spread[:].rearrange("p (q u e) -> p u q e", u=2, e=2))
 
         a, c = FIRST
         d, e = SECOND
         on_scalar, on_vector = nc.scalar.copy, nc.vector.tensor_copy
+        warm_up(3)
+        spread_b(0)
+        spread_b(1)
+        x_grouped[a] = turn_x(a, on_vector, on_scalar)
+        quantise_x(a, x_grouped[a])
+        spread_b(2)
+        spread_b(3)
+        x_grouped[c] = turn_x(c, on_vector, on_scalar)
+        quantise_x(c, x_grouped[c])
+        for j in range(CHUNKS):
+            spread_g_bias(j)
+
         layer1(a, 0)
         layer1(c, 0)
-        spread_g_bias(0)
         layer1(a, 1)
         layer1(c, 1)
-        spread_g_bias(1)
         layer1(a, 2)
         turn_h(a, 0, on_scalar)
         layer1(a, 3)
-        spread_g_bias(2)
         quantise_h(a, 0)
         layer1(c, 2)
         turn_h(a, 1, on_scalar)
-        turn_h(c, 0, on_scalar)
+        turn_h(c, 0, on_vector)
         quantise_h(a, 1)
-        spread_g_bias(3)
         layer1(c, 3)
-        product(0)
-        turn_h(c, 1, on_scalar)
-        x_grouped[d] = turn_x(d, on_scalar)
         quantise_h(c, 0)
-        take_turns(0)
-        take_whole(0)
-        quantise_h(c, 1)
-        take_frac(0)
-        take_cosine(0)
-        quantise_x(d, x_grouped[d])
-        take_size(0)
-        x_grouped[e] = turn_x(e, on_scalar)
-        pair_step(1, d, 0)
-        pair_step(2, d, 1, quantise=lambda: quantise_x(e, x_grouped[e]))
-        pair_step(3, d, 2, turn=lambda: turn_h(d, 0, on_scalar))
-        pair_step(4, d, 3, quantise=lambda: quantise_h(d, 0))
-        pair_step(5, e, 0, turn=lambda: turn_h(d, 1, on_scalar))
-        pair_step(6, e, 1, quantise=lambda: quantise_h(d, 1))
-        pair_step(7, e, 2, turn=lambda: turn_h(e, 0, on_scalar))
-        pair_step(8, e, 3, quantise=lambda: quantise_h(e, 0))
-        product(9)
-        turn_h(e, 1, on_scalar)
-        take_turns(9)
-        take_whole(9)
-        take_sign(8)
-        finish(8, nc.gpsimd.tensor_tensor)
-        product(10)
-        step(10)
-        quantise_h(e, 1)
-        for k in range(11, len(LAYER2_ORDER)):
-            product(k)
-            step(k)
-        for k in range(len(LAYER2_ORDER), len(LAYER2_ORDER) + 2):
-            step(k)
+
+        def begin_second():
+            turn_h(c, 1, on_scalar)
+            x_grouped[d] = turn_x(d, on_scalar, on_scalar)
+
+        def quantise_first():
+            quantise_h(c, 1)
+            quantise_x(d, x_grouped[d])
+
+        def turn_last_x():
+            x_grouped[e] = turn_x(e, on_scalar, on_vector)
+
+        single_step(0, None, begin_second, quantise_first)
+        single_step(1, (d, 0), turn_last_x)
+        single_step(2, (d, 1), None, lambda: quantise_x(e, x_grouped[e]))
+        single_step(3, (d, 2), lambda: turn_h(d, 0, on_scalar))
+        single_step(4, (d, 3), None, lambda: quantise_h(d, 0))
+        single_step(5, (e, 0), lambda: turn_h(d, 1, on_scalar))
+        single_step(6, (e, 1), None, lambda: quantise_h(d, 1))
+        single_step(7, (e, 2), lambda: turn_h(e, 0, on_scalar))
+        single_step(8, (e, 3), None, lambda: quantise_h(e, 0))
+        single_step(9, None, lambda: turn_h(e, 1, on_vector))
+        take_sign(9)
+        double_step(10, lambda: quantise_h(e, 1))
+        double_step(12)
+        double_step(14)
+        for k in range(10, len(LAYER2_ORDER)):
+            multiply(k)

@@ -103,8 +103,8 @@ def tile_onehiddenlayer_kernel(tc, x, W_words, W_scales, b, g_words, g_scales, g
 
         nc.scalar.activation(out=sin_col[:], in_=zero_col[:], func=ACT.Sin)
 
-        def spread_chunk(row):
-            spread = sums.tile([P, CHUNK], F32, tag="sum")
+        def spread_chunk(row, pool, tag):
+            spread = pool.tile([P, CHUNK], F32, name="spread", tag=tag)
             selector = ident_bf16[:, row : row + 1].to_broadcast([P, P])
             nc.tensor.matmul(out=spread[:], lhsT=selector, rhs=bias_rows[:], start=True, stop=True)
             return spread
@@ -188,7 +188,7 @@ def tile_onehiddenlayer_kernel(tc, x, W_words, W_scales, b, g_words, g_scales, g
             )
 
         def spread_g_bias(j):
-            spread = spread_chunk(CHUNKS + j)
+            spread = spread_chunk(CHUNKS + j, turned, "turned")
             nc.scalar.activation(
                 out=g_turns[:, CHUNK * j : CHUNK * (j + 1)], in_=spread[:], func=ACT.Copy, scale=1.0 / TURN, bias=0.25
             )
@@ -235,7 +235,7 @@ def tile_onehiddenlayer_kernel(tc, x, W_words, W_scales, b, g_words, g_scales, g
 
         def finish(k, multiply):
             m, j = LAYER2_ORDER[k]
-            flow[k]["result"] = tail.tile([P, CHUNK], F32, name="result", tag="result")
+            flow[k]["result"] = tail.tile([P, CHUNK], F32, name="result", tag="result", bufs=6)
             multiply(out=flow[k]["result"][:], in0=flow[k]["cosine"][:], in1=flow[k]["sign"][:], op=ALU.mult)
             nc.sync.dma_start(out=out[P * m : P * (m + 1), CHUNK * j : CHUNK * (j + 1)], in_=flow[k]["result"][:])
 
@@ -286,20 +286,18 @@ def tile_onehiddenlayer_kernel(tc, x, W_words, W_scales, b, g_words, g_scales, g
             for i in both:
                 take_sign(i)
         def spread_b(j):
-            spread = spread_chunk(j)
+            spread = spread_chunk(j, sums, "sum")
             nc.scalar.copy(out=b_sorted[:, j, :, :, :], in_=spread[:].rearrange("p (q u e) -> p u q e", u=2, e=2))
 
         a, c = FIRST
         d, e = SECOND
         on_scalar, on_vector = nc.scalar.copy, nc.vector.tensor_copy
-        warm_up(3)
-        spread_b(0)
-        spread_b(1)
-        x_grouped[a] = turn_x(a, on_vector, on_scalar)
+        warm_up(4)
+        x_grouped[a] = turn_x(a, on_vector, on_vector)
         quantise_x(a, x_grouped[a])
-        spread_b(2)
-        spread_b(3)
-        x_grouped[c] = turn_x(c, on_vector, on_scalar)
+        for j in range(CHUNKS):
+            spread_b(j)
+        x_grouped[c] = turn_x(c, on_vector, on_vector)
         quantise_x(c, x_grouped[c])
         for j in range(CHUNKS):
             spread_g_bias(j)

@@ -43,8 +43,8 @@ def tile_onehiddenlayer_kernel(tc, x, W_words, W_scales, b, g_words, g_scales, g
 
         bias_rows = keep.tile([P, CHUNK], BF16)
         idle = keep.tile([P, CHUNK], BF16)
-        w_planes = keep.tile([P, D], U8, align_bytes=64)
-        g_planes = keep.tile([P, D], U8, align_bytes=64)
+        w_planes = keep.tile([P, D], U8, align_bytes=256)
+        g_planes = keep.tile([P, D], U8, align_bytes=256)
         zero_col = keep.tile([P, 1], F32)
         sin_col = keep.tile([P, 1], F32)
         neg_eps = keep.tile([P, 1], F32)
@@ -53,12 +53,12 @@ def tile_onehiddenlayer_kernel(tc, x, W_words, W_scales, b, g_words, g_scales, g
         b_sorted = keep.tile([P, CHUNKS, 2, P, 2], F32)
         g_turns = keep.tile([P, D], F32)
         x_rows = [keep.tile([P, D], BF16, name="x_rows%d" % m) for m in range(TILES)]
-        w_chunks = [keep.tile([P, GROUPS, CHUNK], U32, name="w_chunk%d" % j, align_bytes=64) for j in range(CHUNKS)]
-        g_chunks = [keep.tile([P, GROUPS, CHUNK], U32, name="g_chunk%d" % j, align_bytes=64) for j in range(CHUNKS)]
-        x_codes = [keep.tile([P, GROUPS, P], U32, name="x_codes%d" % m, align_bytes=64) for m in range(TILES)]
-        x_scales = [keep.tile([P, GROUPS, P], U8, name="x_scales%d" % m, align_bytes=64) for m in range(TILES)]
-        h_codes = [keep.tile([P, GROUPS, P], U32, name="h_codes%d" % m, align_bytes=64) for m in range(TILES)]
-        h_scales = [keep.tile([P, GROUPS, P], U8, name="h_scales%d" % m, align_bytes=64) for m in range(TILES)]
+        w_chunks = [keep.tile([P, GROUPS, CHUNK], U32, name="w_chunk%d" % j, align_bytes=256) for j in range(CHUNKS)]
+        g_chunks = [keep.tile([P, GROUPS, CHUNK], U32, name="g_chunk%d" % j, align_bytes=256) for j in range(CHUNKS)]
+        x_codes = [keep.tile([P, GROUPS, P], U32, name="x_codes%d" % m, align_bytes=256) for m in range(TILES)]
+        x_scales = [keep.tile([P, GROUPS, P], U8, name="x_scales%d" % m, align_bytes=256) for m in range(TILES)]
+        h_codes = [keep.tile([P, GROUPS, P], U32, name="h_codes%d" % m, align_bytes=256) for m in range(TILES)]
+        h_scales = [keep.tile([P, GROUPS, P], U8, name="h_scales%d" % m, align_bytes=256) for m in range(TILES)]
 
         nc.vector.memset(zero_col[:], 0.0)
         nc.vector.memset(bias_rows[:].bitcast(I32), 0)
@@ -116,7 +116,7 @@ def tile_onehiddenlayer_kernel(tc, x, W_words, W_scales, b, g_words, g_scales, g
 
         def turn_x(m, first_copy, second_copy):
             words = x_rows[m][:].bitcast(F32)
-            grouped = stage.tile([P, GROUPS, P, PACK], BF16, align_bytes=64, tag="x_grouped", bufs=2)
+            grouped = stage.tile([P, GROUPS, P, PACK], BF16, align_bytes=256, tag="x_grouped", bufs=2)
             for half in range(2):
                 bank = turned.tile([P, 2, 2, P], F32, tag="turned")
                 for g2 in range(2):
@@ -177,7 +177,7 @@ def tile_onehiddenlayer_kernel(tc, x, W_words, W_scales, b, g_words, g_scales, g
                 for u in range(2):
                     first = P * (2 * j2 + u)
                     nc.tensor.transpose(bank[:, j2, u, :], words[:, first : first + P], ident_f32[:])
-            h_grouped[(m, pair)] = stage.tile([P, 2, P, PACK], BF16, align_bytes=64, name="h_grouped", tag="h_grouped")
+            h_grouped[(m, pair)] = stage.tile([P, 2, P, PACK], BF16, align_bytes=256, name="h_grouped", tag="h_grouped")
             copy(out=h_grouped[(m, pair)][:].bitcast(F32), in_=bank[:].rearrange("p j u r -> p j r u"))
 
         def quantise_h(m, pair):

import math
from contextlib import ExitStack

import concourse.mybir as mybir
from concourse.masks import make_identity

FLOPS = 2 * 2 * 512 * 2048 * 2048

F32 = mybir.dt.float32
BF16 = mybir.dt.bfloat16
I32 = mybir.dt.int32
U32 = mybir.dt.uint32
U8 = mybir.dt.uint8
FP8X4 = mybir.dt.float8_e4m3fn_x4
ALU = mybir.AluOpType
ACT = mybir.ActivationFunctionType

P = 128
PACK = 4
K_PASS = P * PACK
CHUNK = 512
BATCH, D = 512, 2048
TILES = BATCH // P
GROUPS = D // K_PASS
CHUNKS = D // CHUNK
EPS = 0.01
TURN = 2.0 * math.pi

FIRST, SECOND = (0, 1), (2, 3)
ON_GPSIMD = range(8)
LAYER2_ORDER = [(m, j) for j in range(CHUNKS) for m in FIRST] + [(m, j) for m in SECOND for j in range(CHUNKS)]


def tile_onehiddenlayer_kernel(tc, x, W_words, W_scales, b, g_words, g_scales, g_bias, out):
    nc = tc.nc
    with ExitStack() as ctx:
        ctx.enter_context(tc.manual_schedule())
        keep = ctx.enter_context(tc.tile_pool(name="keep", bufs=1))
        stage = ctx.enter_context(tc.tile_pool(name="stage", bufs=4))
        tail = ctx.enter_context(tc.tile_pool(name="tail", bufs=4))
        sums = ctx.enter_context(tc.psum_pool(name="sums", bufs=4))
        turned = ctx.enter_context(tc.psum_pool(name="turned", bufs=4))

        bias_rows = keep.tile([P, CHUNK], BF16)
        idle = keep.tile([P, CHUNK], BF16)
        w_planes = keep.tile([P, D], U8, align_bytes=256)
        g_planes = keep.tile([P, D], U8, align_bytes=256)
        zero_col = keep.tile([P, 1], F32)
        sin_col = keep.tile([P, 1], F32)
        neg_eps = keep.tile([P, 1], F32)
        ident_f32 = keep.tile([P, P], F32)
        ident_bf16 = keep.tile([P, P], BF16)
        b_sorted = keep.tile([P, CHUNKS, 2, P, 2], F32)
        g_turns = keep.tile([P, D], F32)
        x_rows = [keep.tile([P, D], BF16, name="x_rows%d" % m) for m in range(TILES)]
        w_chunks = [keep.tile([P, GROUPS, CHUNK], U32, name="w_chunk%d" % j, align_bytes=256) for j in range(CHUNKS)]
        g_chunks = [keep.tile([P, GROUPS, CHUNK], U32, name="g_chunk%d" % j, align_bytes=256) for j in range(CHUNKS)]
        x_codes = [keep.tile([P, GROUPS, P], U32, name="x_codes%d" % m, align_bytes=256) for m in range(TILES)]
        x_scales = [keep.tile([P, GROUPS, P], U8, name="x_scales%d" % m, align_bytes=256) for m in range(TILES)]
        h_codes = [keep.tile([P, GROUPS, P], U32, name="h_codes%d" % m, align_bytes=256) for m in range(TILES)]
        h_scales = [keep.tile([P, GROUPS, P], U8, name="h_scales%d" % m, align_bytes=256) for m in range(TILES)]

        nc.vector.memset(zero_col[:], 0.0)
        nc.vector.memset(bias_rows[:].bitcast(I32), 0)
        nc.vector.memset(idle[:].bitcast(I32), 0)
        nc.vector.memset(w_planes[:].bitcast(I32), 0)
        make_identity(nc, ident_f32[:])
        nc.vector.tensor_copy(out=ident_bf16[:], in_=ident_f32[:])
        nc.vector.memset(neg_eps[:], -EPS)
        nc.vector.memset(g_planes[:].bitcast(I32), 0)

        def load_planes(planes, scales):
            for quadrant in range(4):
                nc.sync.dma_start(
                    out=planes[32 * quadrant : 32 * quadrant + 16, :].bitcast(I32),
                    in_=scales[:, 4 * quadrant : 4 * quadrant + 4, :].bitcast(I32),
                )

        def load_chunk(chunk_tile, words, j):
            by_partition = words.rearrange("g p n t -> p g (n t)")
            nc.sync.dma_start(
                out=chunk_tile[:].bitcast(I32),
                in_=by_partition[:, :, PACK * CHUNK * j : PACK * CHUNK * (j + 1)].bitcast(I32),
            )

        def load_x(m):
            nc.sync.dma_start(out=x_rows[m][:], in_=x[P * m : P * (m + 1), :])

        nc.scalar.dma_start(out=bias_rows[0:CHUNKS, :], in_=b.rearrange("(j n) -> j n", j=CHUNKS))
        nc.scalar.dma_start(out=bias_rows[CHUNKS : 2 * CHUNKS, :], in_=g_bias.rearrange("(j n) -> j n", j=CHUNKS))
        load_x(FIRST[0])
        load_x(FIRST[1])
        load_planes(w_planes, W_scales)
        for j in range(CHUNKS):
            load_chunk(w_chunks[j], W_words, j)
        load_planes(g_planes, g_scales)
        load_chunk(g_chunks[0], g_words, 0)
        load_x(SECOND[0])
        load_chunk(g_chunks[1], g_words, 1)
        load_x(SECOND[1])
        for j in range(2, CHUNKS):
            load_chunk(g_chunks[j], g_words, j)

        nc.scalar.activation(out=sin_col[:], in_=zero_col[:], func=ACT.Sin)

        def spread_chunk(row, pool, tag):
            spread = pool.tile([P, CHUNK], F32, name="spread", tag=tag)
            selector = ident_bf16[:, row : row + 1].to_broadcast([P, P])
            nc.tensor.matmul(out=spread[:], lhsT=selector, rhs=bias_rows[:], start=True, stop=True)
            return spread

        def warm_up(passes):
            spare = sums.tile([P, CHUNK], F32, tag="sum")
            for i in range(passes):
                nc.tensor.matmul(out=spare[:], lhsT=idle[:, 0:P], rhs=idle[:], start=True, stop=True)

        def turn_x(m, first_copy, second_copy):
            words = x_rows[m][:].bitcast(F32)
            grouped = stage.tile([P, GROUPS, P, PACK], BF16, align_bytes=256, tag="x_grouped", bufs=2)
            for half in range(2):
                bank = turned.tile([P, 2, 2, P], F32, tag="turned")
                for g2 in range(2):
                    g = 2 * half + g2
                    for u in range(2):
                        nc.tensor.transpose(bank[:, g2, u, :], words[:, 256 * g + u : 256 * (g + 1) : 2], ident_f32[:])
                copy = first_copy if half == 0 else second_copy
                copy(out=grouped[:].bitcast(F32)[:, 2 * half : 2 * half + 2, :, :], in_=bank[:].rearrange("p g u r -> p g r u"))
            return grouped

        def quantise_x(m, grouped):
            nc.vector.quantize_mx(
                out=x_codes[m][:].rearrange("p g r -> p (g r)").bitcast(FP8X4),
                scales=x_scales[m][:].rearrange("p g r -> p (g r)"),
                in_=grouped[:].rearrange("p g r t -> p (g r t)"),
            )

        def mx_product(codes, scales, chunk_tile, planes, j):
            acc = sums.tile([P, CHUNK], F32, tag="sum")
            for g in range(GROUPS):
                nc.tensor.matmul_mx(
                    out=acc[:],
                    lhsT=codes[:, g, :].bitcast(FP8X4),
                    lhsT_scale=scales[:, g, :],
                    rhs=chunk_tile[:, g, :].bitcast(FP8X4),
                    rhs_scale=planes[4 * g : P, CHUNK * j : CHUNK * (j + 1)],
                    start=(g == 0),
                    stop=(g == GROUPS - 1),
                )
            return acc

        h_sorted, h_grouped, x_grouped = {}, {}, {}

        layer1_sums = {}

        def layer1_product(m, j):
            layer1_sums[(m, j)] = mx_product(x_codes[m], x_scales[m], w_chunks[j], w_planes, j)

        def layer1_add(m, j):
            acc = layer1_sums[(m, j)]
            if j % 2 == 0:
                h_sorted[(m, j // 2)] = stage.tile([P, 2, 2, P, 2], BF16, name="h_sorted", tag="h_sorted")
            nc.vector.tensor_tensor(
                out=h_sorted[(m, j // 2)][:, j % 2, :, :, :],
                in0=acc[:].rearrange("p (q u e) -> p u q e", u=2, e=2),
                in1=b_sorted[:, j, :, :, :],
                op=ALU.add,
            )

        def layer1(m, j):
            layer1_product(m, j)
            layer1_add(m, j)

        def turn_h(m, pair, copy):
            words = h_sorted[(m, pair)][:].rearrange("p j u q e -> p (j u q e)").bitcast(F32)
            bank = turned.tile([P, 2, 2, P], F32, tag="turned")
            for j2 in range(2):
                for u in range(2):
                    first = P * (2 * j2 + u)
                    nc.tensor.transpose(bank[:, j2, u, :], words[:, first : first + P], ident_f32[:])
            h_grouped[(m, pair)] = stage.tile([P, 2, P, PACK], BF16, align_bytes=256, name="h_grouped", tag="h_grouped")
            copy(out=h_grouped[(m, pair)][:].bitcast(F32), in_=bank[:].rearrange("p j u r -> p j r u"))

        def quantise_h(m, pair):
            nc.vector.quantize_mx(
                out=h_codes[m][:, 2 * pair : 2 * pair + 2, :].rearrange("p g r -> p (g r)").bitcast(FP8X4),
                scales=h_scales[m][:, 2 * pair : 2 * pair + 2, :].rearrange("p g r -> p (g r)"),
                in_=h_grouped[(m, pair)][:].rearrange("p j r t -> p (j r t)"),
            )

        def spread_g_bias(j):
            spread = spread_chunk(CHUNKS + j, turned, "turned")
            nc.scalar.activation(
                out=g_turns[:, CHUNK * j : CHUNK * (j + 1)], in_=spread[:], func=ACT.Copy, scale=1.0 / TURN, bias=0.25
            )

        flow = {}

        def product(k):
            m, j = LAYER2_ORDER[k]
            flow[k] = {"sum": mx_product(h_codes[m], h_scales[m], g_chunks[j], g_planes, j)}

        def take_turns(k):
            m, j = LAYER2_ORDER[k]
            flow[k]["turns"] = tail.tile([P, CHUNK], F32, name="turns", tag="turns")
            nc.vector.scalar_tensor_tensor(
                out=flow[k]["turns"][:],
                in0=flow[k]["sum"][:],
                scalar=1.0 / TURN,
                in1=g_turns[:, CHUNK * j : CHUNK * (j + 1)],
                op0=ALU.mult,
                op1=ALU.add,
            )

        def take_whole(k):
            flow[k]["whole"] = tail.tile([P, CHUNK], I32, name="whole", tag="whole")
            nc.vector.tensor_copy(out=flow[k]["whole"][:], in_=flow[k]["turns"][:])

        def take_frac(k):
            flow[k]["frac"] = tail.tile([P, CHUNK], F32, name="frac", tag="frac")
            nc.vector.tensor_tensor(
                out=flow[k]["frac"][:], in0=flow[k]["turns"][:], in1=flow[k]["whole"][:], op=ALU.subtract
            )

        def take_cosine(k):
            flow[k]["cosine"] = tail.tile([P, CHUNK], F32, name="cosine", tag="cosine", bufs=8)
            nc.scalar.activation(out=flow[k]["cosine"][:], in_=flow[k]["frac"][:], func=ACT.Sin, scale=TURN)

        def take_size(k):
            flow[k]["size"] = tail.tile([P, CHUNK], F32, name="size", tag="size")
            nc.scalar.activation(out=flow[k]["size"][:], in_=flow[k]["cosine"][:], func=ACT.Abs)

        def take_sign(k):
            flow[k]["sign"] = tail.tile([P, CHUNK], F32, name="keep_sign", tag="keep_sign", bufs=8)
            nc.scalar.activation(out=flow[k]["sign"][:], in_=flow[k]["size"][:], func=ACT.Sign, bias=neg_eps[:])

        def finish(k, multiply):
            m, j = LAYER2_ORDER[k]
            flow[k]["result"] = tail.tile([P, CHUNK], F32, name="result", tag="result", bufs=6)
            multiply(out=flow[k]["result"][:], in0=flow[k]["cosine"][:], in1=flow[k]["sign"][:], op=ALU.mult)
            nc.sync.dma_start(out=out[P * m : P * (m + 1), CHUNK * j : CHUNK * (j + 1)], in_=flow[k]["result"][:])

        def multiply(k):
            finish(k, nc.gpsimd.tensor_tensor if k in ON_GPSIMD else nc.vector.tensor_tensor)

        def single_step(k, other=None, turn=None, quantise=None):
            product(k)
            if turn:
                turn()
            if other:
                layer1_product(*other)
            take_turns(k)
            if other:
                layer1_add(*other)
            take_whole(k)
            if quantise:
                quantise()
            if k >= 3 and k - 3 not in ON_GPSIMD:
                multiply(k - 3)
            take_frac(k)
            take_cosine(k)
            take_size(k)
            if k >= 1:
                take_sign(k - 1)
                if k - 1 in ON_GPSIMD:
                    multiply(k - 1)

        def double_step(k, quantise=None):
            both = (k, k + 1)
            for i in both:
                product(i)
            if quantise:
                quantise()
            for i in (k - 6, k - 5):
                if i not in ON_GPSIMD:
                    multiply(i)
            for i in both:
                take_turns(i)
            for i in both:
                take_whole(i)
            for i in both:
                take_frac(i)
            for i in both:
                take_cosine(i)
            for i in both:
                take_size(i)
            for i in both:
                take_sign(i)
        def spread_b(j):
            spread = spread_chunk(j, sums, "sum")
            nc.scalar.copy(out=b_sorted[:, j, :, :, :], in_=spread[:].rearrange("p (q u e) -> p u q e", u=2, e=2))

        a, c = FIRST
        d, e = SECOND
        on_scalar, on_vector = nc.scalar.copy, nc.vector.tensor_copy
        warm_up(4)
        x_grouped[a] = turn_x(a, on_vector, on_vector)
        quantise_x(a, x_grouped[a])
        for j in range(CHUNKS):
            spread_b(j)
        x_grouped[c] = turn_x(c, on_vector, on_vector)
        quantise_x(c, x_grouped[c])
        for j in range(CHUNKS):
            spread_g_bias(j)

        layer1(a, 0)
        layer1(c, 0)
        layer1(a, 1)
        layer1(c, 1)
        layer1(a, 2)
        turn_h(a, 0, on_scalar)
        layer1(a, 3)
        quantise_h(a, 0)
        layer1(c, 2)
        turn_h(a, 1, on_scalar)
        turn_h(c, 0, on_vector)
        quantise_h(a, 1)
        layer1(c, 3)
        quantise_h(c, 0)

        def begin_second():
            turn_h(c, 1, on_scalar)
            x_grouped[d] = turn_x(d, on_scalar, on_scalar)

        def quantise_first():
            quantise_h(c, 1)
            quantise_x(d, x_grouped[d])

        def turn_last_x():
            x_grouped[e] = turn_x(e, on_scalar, on_vector)

        single_step(0, None, begin_second, quantise_first)
        single_step(1, (d, 0), turn_last_x)
        single_step(2, (d, 1), None, lambda: quantise_x(e, x_grouped[e]))
        single_step(3, (d, 2), lambda: turn_h(d, 0, on_scalar))
        single_step(4, (d, 3), None, lambda: quantise_h(d, 0))
        single_step(5, (e, 0), lambda: turn_h(d, 1, on_scalar))
        single_step(6, (e, 1), None, lambda: quantise_h(d, 1))
        single_step(7, (e, 2), lambda: turn_h(e, 0, on_scalar))
        single_step(8, (e, 3), None, lambda: quantise_h(e, 0))
        single_step(9, None, lambda: turn_h(e, 1, on_vector))
        take_sign(9)
        double_step(10, lambda: quantise_h(e, 1))
        double_step(12)
        double_step(14)
        for k in range(10, len(LAYER2_ORDER)):
            multiply(k)
